import numpy as np
import ml_dtypes


def mxq(x, axis, fmt="e4m3"):
    dtype, down = {"e4m3": (ml_dtypes.float8_e4m3fn, 7), "e5m2": (ml_dtypes.float8_e5m2, 14)}[fmt]
    v = np.moveaxis(np.asarray(x, np.float32).astype(ml_dtypes.bfloat16).astype(np.float64), axis, -1)
    blocks = v.reshape(v.shape[:-1] + (-1, 32))
    amax = np.abs(blocks).max(-1, keepdims=True)
    byte = np.maximum(np.where(amax > 0, np.frexp(amax)[1] - 1 + 127, 0) - down, 1)
    scale = np.exp2(byte - 127.0)
    codes = (blocks / scale).astype(np.float32).astype(dtype).astype(np.float64)
    return np.moveaxis((codes * scale).reshape(v.shape), -1, axis)


WIDE = False


def mx_kscale(k):
    if not WIDE:
        return np.ones(k)
    levels = np.array([10, -10, 5, -5, 0])
    if k % 512:
        return np.exp2(np.random.permutation(np.resize(levels, k // 32))).repeat(32)
    a = np.empty((k // 512, 16))
    for p in range(k // 512):
        a[p, :8] = np.random.permutation(np.resize(levels, 8))
        for g in range(8):
            far = levels[np.abs(levels - a[p, g]) >= 10]
            a[p, g + 8] = far[np.random.randint(len(far))]
    return np.exp2(a.ravel()).repeat(32)


BF16 = ml_dtypes.bfloat16


def bf(x):
    return np.asarray(x, np.float32).astype(BF16)


def f64(x):
    return np.asarray(x).astype(np.float64)


E2M1 = np.array([0.0, 0.5, 1.0, 1.5, 2.0, 3.0, 4.0, 6.0, -0.0, -0.5, -1.0, -1.5, -2.0, -3.0, -4.0, -6.0])


def pack_weight(w, fmt):
    k, n = w.shape
    w = f64(bf(w)).reshape(k // 32, 32, n)
    amax = np.abs(w).max(1)
    if fmt == "e4m3":
        byte = np.frexp(amax)[1] - 1 + 127 - 7
    else:
        mant, ex = np.frexp(amax / 6.0)
        byte = np.where(mant > 0.5, ex, ex - 1) + 127
    byte = np.clip(np.where(amax > 0, byte, 1), 1, 254)
    scaled = (w * np.exp2(127.0 - byte)[:, None, :]).reshape(k, n).astype(np.float32)
    by_word = np.ascontiguousarray(scaled.reshape(k // 512, 128, 4, n).transpose(0, 1, 3, 2))
    if fmt == "e4m3":
        words = by_word.astype(ml_dtypes.float8_e4m3fn).view(np.uint8)
    else:
        c = by_word.astype(ml_dtypes.float4_e2m1fn).view(np.uint8) & 0xF
        words = c[..., 0::2] | (c[..., 1::2] << 4)
    return np.ascontiguousarray(words), np.ascontiguousarray(byte.astype(np.uint8).reshape(k // 512, 16, n))


def unpack_weight(words, scales, fmt):
    g, p, n, _ = words.shape
    if fmt == "e4m3":
        vals = np.ascontiguousarray(words).view(ml_dtypes.float8_e4m3fn).astype(np.float64)
    else:
        nib = np.empty((g, p, n, 4), np.uint8)
        nib[..., 0::2] = words & 0xF
        nib[..., 1::2] = words >> 4
        vals = E2M1[nib]
    vals = vals * np.repeat(np.exp2(scales.astype(np.float64) - 127.0), 8, axis=1)[..., None]
    return vals.transpose(0, 1, 3, 2).reshape(g * 512, n)
def pack4(w):
    words, scales = pack_weight(w, "e2m1")
    return words.reshape(words.shape[0], 128, -1), scales


def unpack4(words, scales):
    return unpack_weight(words.reshape(words.shape[0], 128, -1, 2), scales, "e2m1")


B, S, N, D = 2, 2, 1024, 512


def draw0():
    s, t = mx_kscale(D), mx_kscale(D)
    tensor0 = bf(np.random.standard_normal((S, N, D)) * s)
    tensor1 = bf(np.random.standard_normal((S, N, D)) * 0.5 / t)
    kernel = np.random.standard_normal((D, D)) * D ** -0.75 * t[:, None] / s[None, :]
    kernel_words, kernel_scales = pack4(kernel.T)
    return {"tensor0": tensor0,
            "tensor1": tensor1,
            "kernel_words": kernel_words,
            "kernel_scales": kernel_scales,
            "bias": bf(0.5 + 0.1 * np.random.standard_normal(1))}


def core(tensor0, tensor1, kernel_words, kernel_scales, bias):
    q = mxq(f64(tensor0), 2, "e4m3") @ unpack4(kernel_words, kernel_scales)
    out = mxq(f64(tensor1), 2, "e4m3") @ mxq(q, 2, "e4m3").transpose(0, 2, 1)
    out = out + f64(bias)
    return np.ascontiguousarray(np.broadcast_to(out[None], (B,) + out.shape))


def e4m3fn_bytes(y):
    return np.clip(np.asarray(y, np.float64), -448.0, 448.0).astype(np.float32).astype(ml_dtypes.float8_e4m3fn).view(np.uint8)


def e4m3fn_values(b):
    return np.asarray(b, np.uint8).view(ml_dtypes.float8_e4m3fn).astype(np.float64)


def setup_inputs():
    d = draw0()
    x0 = np.asarray(d['tensor1']).astype(np.float64)
    s = (np.max(np.abs(x0), axis=(0, 1), keepdims=True) / 448.0).astype(np.float32)
    out = {}
    for k, v in d.items():
        if k == 'tensor1':
            out['tensor1_bytes'] = e4m3fn_bytes(x0 / s.astype(np.float64))
            out['tensor1_scale'] = s
        else:
            out[k] = v
    return out


def reference(tensor0, tensor1_bytes, tensor1_scale, kernel_words, kernel_scales, bias):
    return core(tensor0, e4m3fn_values(tensor1_bytes) * tensor1_scale.astype(np.float64), kernel_words, kernel_scales, bias)

@@ -1,0 +1,356 @@
+from contextlib import ExitStack
+
+import concourse.mybir as mybir
+from concourse.masks import make_identity
+
+F32 = mybir.dt.float32
+BF16 = mybir.dt.bfloat16
+I32 = mybir.dt.int32
+U32 = mybir.dt.uint32
+U16 = mybir.dt.uint16
+U8 = mybir.dt.uint8
+FP8 = mybir.dt.float8_e4m3fn
+FP8X4 = mybir.dt.float8_e4m3fn_x4
+FP4X4 = mybir.dt.float4_e2m1fn_x4
+ALU = mybir.AluOpType
+ACT = mybir.ActivationFunctionType
+
+B, S, N, D = 2, 2, 1024, 512
+P = 128
+PACK = 4
+ROWS = N // P
+QUARTER = 256
+HALF = 512
+FLOPS = 2 * S * N * D * D + 2 * S * N * N * D
+
+
+def tile_bilinear_w4_kernel(tc, tensor0, tensor1_bytes, tensor1_scale, kernel_words, kernel_scales, bias, out):
+    nc = tc.nc
+    with ExitStack() as ctx:
+        keep = ctx.enter_context(tc.tile_pool(name="keep", bufs=1))
+        work = ctx.enter_context(tc.tile_pool(name="work", bufs=4))
+        psum = ctx.enter_context(tc.psum_pool(name="psum", bufs=8))
+        ctx.enter_context(tc.manual_schedule())
+
+        t0_rows, t1_rows = {}, {}
+
+        def load_t0(s, first, count):
+            raw = keep.tile([P, count, 2, D], BF16, name="t0_raw_%d_%d" % (s, first))
+            rows = tensor0[s, first * QUARTER : (first + count) * QUARTER, :]
+            nc.sync.dma_start(out=raw[:], in_=rows.rearrange("(c p r) e -> p c r e", p=P, r=2))
+            for c in range(count):
+                t0_rows[(s, first + c)] = raw[:, c, :, :]
+
+        def load_t1(s, first, count):
+            raw = keep.tile([P, count, 2, D], U8, name="t1_bytes_%d_%d" % (s, first))
+            rows = tensor1_bytes[s].rearrange("(p g r) d -> p g r d", p=P, r=2)
+            nc.sync.dma_start(out=raw[:], in_=rows[:, first : first + count, :, :])
+            for g in range(count):
+                t1_rows[(s, first + g)] = raw[:, g, :, :]
+
+        w_scale_rows = keep.tile([4, 4, D // 4], I32, name="w_scale_rows")
+        t1_scale = keep.tile([P, PACK], F32, name="t1_scale")
+        w_words_raw = keep.tile([P, D // 2], I32, name="w_words_raw")
+        bias_bf16 = keep.tile([P, 1], BF16, name="bias_bf16")
+        identity = keep.tile([P, P], F32, name="identity")
+        w_scale_spread = keep.tile([P, D // 4], I32, name="w_scale_spread")
+        w_scales = keep.tile([P, D], U8, name="w_scales", align_bytes=64)
+        w_words = keep.tile([P, D], U16, name="w_words", align_bytes=64)
+        t1_scale_row = keep.tile([P, D], F32, name="t1_scale_row")
+
+        def load_w_scales():
+            nc.sync.dma_start(out=w_scale_rows[:], in_=kernel_scales[0].bitcast(I32).rearrange("(q r) n -> r q n", r=4))
+
+        def load_t1_scale():
+            nc.sync.dma_start(out=t1_scale[:], in_=tensor1_scale.rearrange("a b (p t) -> p (a b t)", t=PACK))
+
+        def load_w_words():
+            nc.sync.dma_start(out=w_words_raw[:], in_=kernel_words[0].bitcast(I32))
+
+        def load_bias():
+            nc.sync.dma_start(out=bias_bf16[:], in_=bias.partition_broadcast(P))
+
+        def order_w_scales():
+            nc.vector.memset(w_scale_spread[:], 0)
+            for q in range(4):
+                nc.vector.tensor_copy(out=w_scale_spread[32 * q : 32 * q + 4, :], in_=w_scale_rows[:, q, :])
+            nc.vector.tensor_copy(
+                out=w_scales[:].rearrange("p (t m) -> p m t", t=PACK),
+                in_=w_scale_spread[:].bitcast(U8).rearrange("p (m t) -> p m t", t=PACK),
+            )
+
+        def order_w_words():
+            nc.scalar.copy(
+                out=w_words[:].rearrange("p (t m) -> p t m", t=PACK),
+                in_=w_words_raw[:].bitcast(U16).rearrange("p (m t) -> p t m", t=PACK),
+            )
+
+        def spread_t1_scale():
+            bank = psum.tile([P, HALF], F32, name="bank")
+            for t in range(PACK):
+                nc.tensor.transpose(bank[:, t * P : (t + 1) * P], t1_scale[:, t : t + 1].to_broadcast([P, P]), identity[:])
+            nc.scalar.activation(
+                out=t1_scale_row[:].rearrange("p (u n e) -> p u n e", u=2, e=2),
+                in_=bank[:].rearrange("p (u e n) -> p u n e", u=2, e=2),
+                func=ACT.Identity,
+            )
+
+        banks, grouped, wide = {}, {}, {}
+        codes, scales = {}, {}
+        for s in range(S):
+            for name in ("t0", "t1", "q"):
+                for h in range(2):
+                    codes[(name, s, h)] = keep.tile([P, HALF], U32, name="%s_codes_%d_%d" % (name, s, h), align_bytes=64)
+                    scales[(name, s, h)] = keep.tile([P, HALF], U8, name="%s_scales_%d_%d" % (name, s, h), align_bytes=64)
+        result = {}
+        for s in range(S):
+            for r in range(ROWS):
+                result[(s, r)] = keep.tile([P, N], F32, name="result_%d_%d" % (s, r))
+
+        def operand(name, s, first, count):
+            h, cols = first // HALF, slice(first % HALF, first % HALF + count)
+            return codes[(name, s, h)][:, cols].bitcast(FP8X4), scales[(name, s, h)][:, cols]
+
+        def copy_out(on_vector, dst, src):
+            if on_vector:
+                nc.vector.tensor_copy(out=dst, in_=src)
+            else:
+                nc.scalar.copy(out=dst, in_=src)
+
+        def quantize(name, s, c):
+            words, exps = operand(name, s, c * QUARTER, QUARTER)
+            nc.vector.quantize_mx(out=words, scales=exps, in_=grouped[(name, s, c)][:])
+
+        def turn_t0(s, c):
+            bank = psum.tile([P, HALF], F32, name="bank")
+            banks[("t0", s, c)] = bank
+            words = t0_rows[(s, c)].bitcast(F32)
+            for r in range(2):
+                for u in range(2):
+                    k = 2 * r + u
+                    nc.tensor.transpose(bank[:, k * P : (k + 1) * P], words[:, r, u : D // 2 : 2], identity[:])
+
+        def empty_t0(s, c, on_vector):
+            tile = work.tile([P, QUARTER * PACK], BF16, name="t0_grouped", align_bytes=64)
+            grouped[("t0", s, c)] = tile
+            copy_out(
+                on_vector,
+                tile[:].bitcast(F32).rearrange("q (p r u) -> q p r u", r=2, u=2),
+                banks[("t0", s, c)][:].rearrange("q (r u p) -> q p r u", r=2, u=2),
+            )
+
+        def widen_t1(s, g, r):
+            if r == 0:
+                wide[(s, g)] = work.tile([P, 2, D], BF16, name="t1_wide", align_bytes=64)
+            nc.vector.tensor_tensor(
+                out=wide[(s, g)][:, r, :].rearrange("p (u n e) -> p u n e", u=2, e=2),
+                in0=t1_rows[(s, g)][:, r, :].bitcast(FP8).rearrange("p (n u e) -> p u n e", u=2, e=2),
+                in1=t1_scale_row[:].rearrange("p (u n e) -> p u n e", u=2, e=2),
+                op=ALU.mult,
+            )
+
+        def turn_t1(s, g):
+            bank = psum.tile([P, HALF], F32, name="bank")
+            banks[("t1", s, g)] = bank
+            words = wide[(s, g)][:].bitcast(F32)
+            for r in range(2):
+                for u in range(2):
+                    k = 2 * r + u
+                    nc.tensor.transpose(bank[:, k * P : (k + 1) * P], words[:, r, u * P : (u + 1) * P], identity[:])
+
+        def empty_t1(s, g, on_vector):
+            tile = work.tile([P, QUARTER * PACK], BF16, name="t1_grouped", align_bytes=64)
+            grouped[("t1", s, g)] = tile
+            copy_out(
+                on_vector,
+                tile[:].bitcast(F32).rearrange("q (r p u) -> q r p u", r=2, u=2),
+                banks[("t1", s, g)][:].rearrange("q (r u p) -> q r p u", r=2, u=2),
+            )
+
+        def multiply_q(s, c, b):
+            bank = psum.tile([P, HALF], F32, name="bank")
+            banks[("q", s, c, b)] = bank
+            words, exps = operand("t0", s, c * QUARTER + b * P, P)
+            for t in range(PACK):
+                nc.tensor.matmul_mx(
+                    out=bank[:, t * P : (t + 1) * P],
+                    lhsT=w_words[:, t * P : (t + 1) * P].bitcast(FP4X4),
+                    lhsT_scale=w_scales[:, t * P : (t + 1) * P],
+                    rhs=words,
+                    rhs_scale=exps,
+                    start=True,
+                    stop=True,
+                )
+
+        def empty_q(s, c, b, on_vector):
+            if b == 0:
+                grouped[("q", s, c)] = work.tile([P, QUARTER * PACK], BF16, name="q_grouped", align_bytes=64)
+            copy_out(
+                on_vector,
+                grouped[("q", s, c)][:, b * HALF : (b + 1) * HALF].rearrange("p (j t) -> p j t", t=PACK),
+                banks[("q", s, c, b)][:].rearrange("p (t j) -> p j t", t=PACK),
+            )
+
+        def multiply_score(s, r, first, count):
+            bank = psum.tile([P, HALF], F32, name="bank")
+            banks[("score", s, r, first)] = bank
+            t1_words, t1_exps = operand("t1", s, r * P, P)
+            q_words, q_exps = operand("q", s, first, count)
+            nc.tensor.matmul_mx(
+                out=bank[:, 0:count], lhsT=t1_words, lhsT_scale=t1_exps, rhs=q_words, rhs_scale=q_exps, start=True, stop=True
+            )
+
+        def empty_score(s, r, first, count, on_vector):
+            dst = result[(s, r)][:, first : first + count]
+            src = banks[("score", s, r, first)][:, 0:count]
+            if on_vector:
+                nc.vector.tensor_scalar_add(out=dst, in0=src, scalar1=bias_bf16[:])
+            else:
+                nc.scalar.activation(out=dst, in_=src, func=ACT.Identity, bias=bias_bf16[:])
+
+        def store(s, r, first, count):
+            rows = out[:, s].rearrange("b (p r) j -> p r b j", r=ROWS)
+            nc.sync.dma_start(
+                out=rows[:, r, :, first : first + count],
+                in_=result[(s, r)][:, first : first + count].unsqueeze(1).to_broadcast([P, B, count]),
+            )
+
+
+        load_w_scales()
+        load_t1_scale()
+        load_t0(0, 0, 1)
+        load_t1(0, 0, 1)
+        load_w_words()
+        load_t0(0, 1, 1)
+        load_t1(0, 1, 3)
+        load_bias()
+        load_t0(0, 2, 2)
+        load_t0(1, 0, 2)
+        load_t0(1, 2, 2)
+        load_t1(1, 0, 4)
+        make_identity(nc, identity[:])
+        order_w_scales()
+        spread_t1_scale()
+
+        def scores(s, rows, first, count):
+            for r in rows:
+                multiply_score(s, r, first, count)
+
+        def finish(s, r, first, count, on_vector):
+            empty_score(s, r, first, count, on_vector)
+            store(s, r, first, count)
+
+        turn_t0(0, 0)
+        empty_t0(0, 0, False)
+        order_w_words()
+        widen_t1(0, 0, 0)
+        widen_t1(0, 0, 1)
+        quantize("t0", 0, 0)
+        turn_t0(0, 1)
+        turn_t1(0, 0)
+        empty_t0(0, 1, False)
+        multiply_q(0, 0, 0)
+        multiply_q(0, 0, 1)
+        empty_t1(0, 0, False)
+        widen_t1(0, 1, 0)
+        quantize("t0", 0, 1)
+        empty_q(0, 0, 0, True)
+        empty_q(0, 0, 1, False)
+        multiply_q(0, 1, 0)
+        multiply_q(0, 1, 1)
+        quantize("t1", 0, 0)
+        quantize("q", 0, 0)
+        widen_t1(0, 1, 1)
+        empty_q(0, 1, 0, False)
+        empty_q(0, 1, 1, False)
+        scores(0, (0, 1), 0, QUARTER)
+        turn_t1(0, 1)
+        finish(0, 0, 0, QUARTER, True)
+        quantize("q", 0, 1)
+        finish(0, 1, 0, QUARTER, False)
+        empty_t1(0, 1, False)
+        widen_t1(0, 2, 0)
+        scores(0, (0, 1), QUARTER, QUARTER)
+        turn_t0(0, 2)
+        quantize("t1", 0, 1)
+        finish(0, 0, QUARTER, QUARTER, False)
+        finish(0, 1, QUARTER, QUARTER, False)
+        widen_t1(0, 2, 1)
+        empty_t0(0, 2, False)
+        scores(0, (2, 3), 0, HALF)
+        turn_t1(0, 2)
+        turn_t0(0, 3)
+        widen_t1(0, 3, 0)
+        finish(0, 2, 0, HALF, False)
+        quantize("t0", 0, 2)
+        finish(0, 3, 0, HALF, True)
+        empty_t1(0, 2, False)
+        widen_t1(0, 3, 1)
+        empty_t0(0, 3, False)
+        quantize("t1", 0, 2)
+        multiply_q(0, 2, 0)
+        multiply_q(0, 2, 1)
+        turn_t1(0, 3)
+        scores(0, (4, 5), 0, HALF)
+        quantize("t0", 0, 3)
+        empty_q(0, 2, 0, False)
+        empty_t1(0, 3, False)
+        finish(0, 4, 0, HALF, True)
+        empty_q(0, 2, 1, False)
+        quantize("t1", 0, 3)
+        finish(0, 5, 0, HALF, True)
+        multiply_q(0, 3, 0)
+        multiply_q(0, 3, 1)
+        scores(0, (6, 7), 0, HALF)
+        turn_t0(1, 0)
+        turn_t0(1, 1)
+        empty_q(0, 3, 0, False)
+        empty_q(0, 3, 1, False)
+        quantize("q", 0, 2)
+        finish(0, 6, 0, HALF, True)
+        empty_t0(1, 0, False)
+        quantize("q", 0, 3)
+        finish(0, 7, 0, HALF, True)
+        quantize("t0", 1, 0)
+        for c in range(4):
+            scores(0, (2 * c, 2 * c + 1), HALF, HALF)
+            multiply_q(1, c, 0)
+            multiply_q(1, c, 1)
+            if c + 2 < 4:
+                turn_t0(1, c + 2)
+            if c == 2:
+                turn_t1(1, 0)
+            if c + 1 < 4:
+                empty_t0(1, c + 1, False)
+            if c == 3:
+                empty_t1(1, 0, False)
+            finish(0, 2 * c, HALF, HALF, True)
+            if c > 0:
+                quantize("q", 1, c - 1)
+            if c + 1 < 4:
+                quantize("t0", 1, c + 1)
+            if c == 3:
+                quantize("t1", 1, 0)
+            empty_q(1, c, 0, False)
+            empty_q(1, c, 1, False)
+            finish(0, 2 * c + 1, HALF, HALF, True)
+            widen_t1(1, c // 2, c % 2)
+        quantize("q", 1, 3)
+        for g in range(4):
+            scores(1, (2 * g, 2 * g + 1), 0, HALF)
+            if g + 1 < 4:
+                turn_t1(1, g + 1)
+            scores(1, (2 * g, 2 * g + 1), HALF, HALF)
+            empty_score(1, 2 * g, 0, HALF, False)
+            empty_score(1, 2 * g + 1, 0, HALF, True)
+            if g + 1 < 4:
+                empty_t1(1, g + 1, False)
+            empty_score(1, 2 * g, HALF, HALF, True)
+            store(1, 2 * g, 0, N)
+            if g + 1 < 4:
+                quantize("t1", 1, g + 1)
+            empty_score(1, 2 * g + 1, HALF, HALF, False)
+            store(1, 2 * g + 1, 0, N)
+            if g + 2 < 4:
+                widen_t1(1, g + 2, 0)
+                widen_t1(1, g + 2, 1)

@@ -59,16 +59,16 @@ def tile_bilinear_w4_kernel(tc, tensor0, tensor1_bytes, tensor1_scale, kernel_wo
         t1_scale_row = keep.tile([P, D], F32, name="t1_scale_row")
 
         def load_w_scales():
-            nc.sync.dma_start(out=w_scale_rows[:], in_=kernel_scales[0].bitcast(I32).rearrange("(q r) n -> r q n", r=4))
+            nc.scalar.dma_start(out=w_scale_rows[:], in_=kernel_scales[0].bitcast(I32).rearrange("(q r) n -> r q n", r=4))
 
         def load_t1_scale():
-            nc.sync.dma_start(out=t1_scale[:], in_=tensor1_scale.rearrange("a b (p t) -> p (a b t)", t=PACK))
+            nc.scalar.dma_start(out=t1_scale[:], in_=tensor1_scale.rearrange("a b (p t) -> p (a b t)", t=PACK))
 
         def load_w_words():
             nc.sync.dma_start(out=w_words_raw[:], in_=kernel_words[0].bitcast(I32))
 
         def load_bias():
-            nc.sync.dma_start(out=bias_bf16[:], in_=bias.partition_broadcast(P))
+            nc.scalar.dma_start(out=bias_bf16[:], in_=bias.partition_broadcast(P))
 
         def order_w_scales():
             nc.vector.memset(w_scale_spread[:], 0)
@@ -104,8 +104,7 @@ def tile_bilinear_w4_kernel(tc, tensor0, tensor1_bytes, tensor1_scale, kernel_wo
                     scales[(name, s, h)] = keep.tile([P, HALF], U8, name="%s_scales_%d_%d" % (name, s, h), align_bytes=64)
         result = {}
         for s in range(S):
-            for r in range(ROWS):
-                result[(s, r)] = keep.tile([P, N], F32, name="result_%d_%d" % (s, r))
+            result[s] = keep.tile([P, ROWS * N], F32, name="result_%d" % s)
 
         def operand(name, s, first, count):
             h, cols = first // HALF, slice(first % HALF, first % HALF + count)
@@ -117,9 +116,40 @@ def tile_bilinear_w4_kernel(tc, tensor0, tensor1_bytes, tensor1_scale, kernel_wo
             else:
                 nc.scalar.copy(out=dst, in_=src)
 
-        def quantize(name, s, c):
-            words, exps = operand(name, s, c * QUARTER, QUARTER)
-            nc.vector.quantize_mx(out=words, scales=exps, in_=grouped[(name, s, c)][:])
+        def quantize(name, s, c, first=0, count=QUARTER):
+            words, exps = operand(name, s, c * QUARTER + first, count)
+            nc.vector.quantize_mx(out=words, scales=exps, in_=grouped[(name, s, c)][:, first * PACK : (first + count) * PACK])
+
+        def multiply_pair(first, count):
+            bank = psum.tile([P, HALF], F32, name="bank")
+            banks[("pair", first)] = bank
+            q_words, q_exps = operand("q", 0, first, count)
+            for r in range(2):
+                t1_words, t1_exps = operand("t1", 0, r * P, P)
+                nc.tensor.matmul_mx(
+                    out=bank[:, r * count : (r + 1) * count],
+                    lhsT=t1_words,
+                    lhsT_scale=t1_exps,
+                    rhs=q_words,
+                    rhs_scale=q_exps,
+                    start=True,
+                    stop=True,
+                )
+
+        def finish_pair(first, count, on_vector):
+            tile = keep.tile([P, 2 * count], F32, name="pair_result_%d" % first)
+            dst = tile[:]
+            src = banks[("pair", first)][:, 0 : 2 * count]
+            if on_vector:
+                nc.vector.tensor_scalar_add(out=dst, in0=src, scalar1=bias_bf16[:])
+            else:
+                nc.scalar.activation(out=dst, in_=src, func=ACT.Identity, bias=bias_bf16[:])
+            rows = out[:, 0].rearrange("b (p r) j -> p r b j", r=ROWS)
+            for r in range(2):
+                nc.sync.dma_start(
+                    out=rows[:, r, :, first : first + count],
+                    in_=tile[:, r * count : (r + 1) * count].unsqueeze(1).to_broadcast([P, B, count]),
+                )
 
         def turn_t0(s, c):
             bank = psum.tile([P, HALF], F32, name="bank")
@@ -201,7 +231,7 @@ def tile_bilinear_w4_kernel(tc, tensor0, tensor1_bytes, tensor1_scale, kernel_wo
             )
 
         def empty_score(s, r, first, count, on_vector):
-            dst = result[(s, r)][:, first : first + count]
+            dst = result[s][:, r * N + first : r * N + first + count]
             src = banks[("score", s, r, first)][:, 0:count]
             if on_vector:
                 nc.vector.tensor_scalar_add(out=dst, in0=src, scalar1=bias_bf16[:])
@@ -209,21 +239,19 @@ def tile_bilinear_w4_kernel(tc, tensor0, tensor1_bytes, tensor1_scale, kernel_wo
                 nc.scalar.activation(out=dst, in_=src, func=ACT.Identity, bias=bias_bf16[:])
 
         def store(s, r, first, count):
-            rows = out[:, s].rearrange("b (p r) j -> p r b j", r=ROWS)
-            nc.sync.dma_start(
-                out=rows[:, r, :, first : first + count],
-                in_=result[(s, r)][:, first : first + count].unsqueeze(1).to_broadcast([P, B, count]),
-            )
+            rows = out[:, s].rearrange("b (p r) j -> p b (r j)", r=ROWS)
+            cols = slice(r * N + first, r * N + first + count)
+            nc.sync.dma_start(out=rows[:, :, cols], in_=result[s][:, cols].unsqueeze(1).to_broadcast([P, B, count]))
 
 
-        load_w_scales()
         load_t1_scale()
+        load_w_scales()
         load_t0(0, 0, 1)
         load_t1(0, 0, 1)
         load_w_words()
         load_t0(0, 1, 1)
-        load_t1(0, 1, 3)
         load_bias()
+        load_t1(0, 1, 3)
         load_t0(0, 2, 2)
         load_t0(1, 0, 2)
         load_t0(1, 2, 2)
@@ -240,77 +268,79 @@ def tile_bilinear_w4_kernel(tc, tensor0, tensor1_bytes, tensor1_scale, kernel_wo
             empty_score(s, r, first, count, on_vector)
             store(s, r, first, count)
 
+        def both_q(s, c):
+            multiply_q(s, c, 0)
+            multiply_q(s, c, 1)
+
+        def widen_pair(s, g):
+            widen_t1(s, g, 0)
+            widen_t1(s, g, 1)
+
         turn_t0(0, 0)
         empty_t0(0, 0, False)
         order_w_words()
-        widen_t1(0, 0, 0)
-        widen_t1(0, 0, 1)
+        widen_pair(0, 0)
         quantize("t0", 0, 0)
         turn_t0(0, 1)
         turn_t1(0, 0)
+        widen_pair(0, 1)
         empty_t0(0, 1, False)
-        multiply_q(0, 0, 0)
-        multiply_q(0, 0, 1)
         empty_t1(0, 0, False)
-        widen_t1(0, 1, 0)
+        both_q(0, 0)
         quantize("t0", 0, 1)
+        quantize("t1", 0, 0)
+        both_q(0, 1)
         empty_q(0, 0, 0, True)
         empty_q(0, 0, 1, False)
-        multiply_q(0, 1, 0)
-        multiply_q(0, 1, 1)
-        quantize("t1", 0, 0)
         quantize("q", 0, 0)
-        widen_t1(0, 1, 1)
+        widen_t1(0, 2, 0)
         empty_q(0, 1, 0, False)
-        empty_q(0, 1, 1, False)
+        empty_q(0, 1, 1, True)
         scores(0, (0, 1), 0, QUARTER)
         turn_t1(0, 1)
-        finish(0, 0, 0, QUARTER, True)
-        quantize("q", 0, 1)
-        finish(0, 1, 0, QUARTER, False)
-        empty_t1(0, 1, False)
-        widen_t1(0, 2, 0)
-        scores(0, (0, 1), QUARTER, QUARTER)
         turn_t0(0, 2)
+        finish(0, 0, 0, QUARTER, False)
+        finish(0, 1, 0, QUARTER, False)
+        quantize("q", 0, 1)
+        empty_t1(0, 1, False)
+        widen_t1(0, 2, 1)
+        scores(0, (0, 1), QUARTER, QUARTER)
+        turn_t1(0, 2)
         quantize("t1", 0, 1)
+        empty_t0(0, 2, False)
         finish(0, 0, QUARTER, QUARTER, False)
         finish(0, 1, QUARTER, QUARTER, False)
-        widen_t1(0, 2, 1)
-        empty_t0(0, 2, False)
         scores(0, (2, 3), 0, HALF)
-        turn_t1(0, 2)
         turn_t0(0, 3)
         widen_t1(0, 3, 0)
-        finish(0, 2, 0, HALF, False)
         quantize("t0", 0, 2)
-        finish(0, 3, 0, HALF, True)
         empty_t1(0, 2, False)
-        widen_t1(0, 3, 1)
-        empty_t0(0, 3, False)
+        finish(0, 2, 0, HALF, True)
+        finish(0, 3, 0, HALF, False)
         quantize("t1", 0, 2)
-        multiply_q(0, 2, 0)
-        multiply_q(0, 2, 1)
-        turn_t1(0, 3)
+        widen_t1(0, 3, 1)
+        both_q(0, 2)
+        empty_t0(0, 3, False)
         scores(0, (4, 5), 0, HALF)
-        quantize("t0", 0, 3)
+        turn_t1(0, 3)
         empty_q(0, 2, 0, False)
-        empty_t1(0, 3, False)
+        quantize("t0", 0, 3)
         finish(0, 4, 0, HALF, True)
+        empty_t1(0, 3, False)
+        finish(0, 5, 0, HALF, True)
         empty_q(0, 2, 1, False)
         quantize("t1", 0, 3)
-        finish(0, 5, 0, HALF, True)
-        multiply_q(0, 3, 0)
-        multiply_q(0, 3, 1)
+        both_q(0, 3)
         scores(0, (6, 7), 0, HALF)
         turn_t0(1, 0)
         turn_t0(1, 1)
-        empty_q(0, 3, 0, False)
-        empty_q(0, 3, 1, False)
         quantize("q", 0, 2)
-        finish(0, 6, 0, HALF, True)
-        empty_t0(1, 0, False)
+        empty_q(0, 3, 0, False)
+        empty_q(0, 3, 1, True)
+        finish(0, 6, 0, HALF, False)
         quantize("q", 0, 3)
-        finish(0, 7, 0, HALF, True)
+        finish(0, 7, 0, HALF, False)
+        empty_t0(1, 0, True)
         quantize("t0", 1, 0)
         for c in range(4):
             scores(0, (2 * c, 2 * c + 1), HALF, HALF)
@@ -334,23 +364,29 @@ def tile_bilinear_w4_kernel(tc, tensor0, tensor1_bytes, tensor1_scale, kernel_wo
             empty_q(1, c, 0, False)
             empty_q(1, c, 1, False)
             finish(0, 2 * c + 1, HALF, HALF, True)
+            if c == 3:
+                quantize("q", 1, 3)
             widen_t1(1, c // 2, c % 2)
-        quantize("q", 1, 3)
         for g in range(4):
             scores(1, (2 * g, 2 * g + 1), 0, HALF)
+            scores(1, (2 * g, 2 * g + 1), HALF, HALF)
             if g + 1 < 4:
                 turn_t1(1, g + 1)
-            scores(1, (2 * g, 2 * g + 1), HALF, HALF)
             empty_score(1, 2 * g, 0, HALF, False)
             empty_score(1, 2 * g + 1, 0, HALF, True)
+            empty_score(1, 2 * g, HALF, HALF, False)
+            if g == 0:
+                store(1, 0, 0, N)
+            empty_score(1, 2 * g + 1, HALF, HALF, True)
+            if g == 0:
+                store(1, 1, 0, N)
+            else:
+                store(1, 2 * g, 0, 2 * N)
             if g + 1 < 4:
                 empty_t1(1, g + 1, False)
-            empty_score(1, 2 * g, HALF, HALF, True)
-            store(1, 2 * g, 0, N)
-            if g + 1 < 4:
-                quantize("t1", 1, g + 1)
-            empty_score(1, 2 * g + 1, HALF, HALF, False)
-            store(1, 2 * g + 1, 0, N)
             if g + 2 < 4:
                 widen_t1(1, g + 2, 0)
+            if g + 1 < 4:
+                quantize("t1", 1, g + 1)
+            if g + 2 < 4:
                 widen_t1(1, g + 2, 1)

@@ -43,7 +43,7 @@ def tile_bilinear_w4_kernel(tc, tensor0, tensor1_bytes, tensor1_scale, kernel_wo
 
         def load_t1(s, first, count):
             raw = keep.tile([P, count, 2, D], U8, name="t1_bytes_%d_%d" % (s, first))
-            rows = tensor1_bytes[s].rearrange("(p g r) d -> p g r d", p=P, r=2)
+            rows = tensor1_bytes[s].rearrange("(g p r) d -> p g r d", p=P, r=2)
             nc.sync.dma_start(out=raw[:], in_=rows[:, first : first + count, :, :])
             for g in range(count):
                 t1_rows[(s, first + g)] = raw[:, g, :, :]
@@ -59,16 +59,16 @@ def tile_bilinear_w4_kernel(tc, tensor0, tensor1_bytes, tensor1_scale, kernel_wo
         t1_scale_row = keep.tile([P, D], F32, name="t1_scale_row")
 
         def load_w_scales():
-            nc.scalar.dma_start(out=w_scale_rows[:], in_=kernel_scales[0].bitcast(I32).rearrange("(q r) n -> r q n", r=4))
+            nc.sync.dma_start(out=w_scale_rows[:], in_=kernel_scales[0].bitcast(I32).rearrange("(q r) n -> r q n", r=4))
 
         def load_t1_scale():
-            nc.scalar.dma_start(out=t1_scale[:], in_=tensor1_scale.rearrange("a b (p t) -> p (a b t)", t=PACK))
+            nc.sync.dma_start(out=t1_scale[:], in_=tensor1_scale.rearrange("a b (p t) -> p (a b t)", t=PACK))
 
         def load_w_words():
             nc.sync.dma_start(out=w_words_raw[:], in_=kernel_words[0].bitcast(I32))
 
         def load_bias():
-            nc.scalar.dma_start(out=bias_bf16[:], in_=bias.partition_broadcast(P))
+            nc.sync.dma_start(out=bias_bf16[:], in_=bias.partition_broadcast(P))
 
         def order_w_scales():
             nc.vector.memset(w_scale_spread[:], 0)
@@ -239,19 +239,20 @@ def tile_bilinear_w4_kernel(tc, tensor0, tensor1_bytes, tensor1_scale, kernel_wo
                 nc.scalar.activation(out=dst, in_=src, func=ACT.Identity, bias=bias_bf16[:])
 
         def store(s, r, first, count):
-            rows = out[:, s].rearrange("b (p r) j -> p b (r j)", r=ROWS)
-            cols = slice(r * N + first, r * N + first + count)
-            nc.sync.dma_start(out=rows[:, :, cols], in_=result[s][:, cols].unsqueeze(1).to_broadcast([P, B, count]))
+            rows = out[:, s].rearrange("b (g p r) j -> g p b (r j)", p=P, r=2)
+            start = (r % 2) * N + first
+            src = result[s][:, r * N + first : r * N + first + count]
+            nc.sync.dma_start(out=rows[r // 2, :, :, start : start + count], in_=src.unsqueeze(1).to_broadcast([P, B, count]))
 
 
-        load_t1_scale()
         load_w_scales()
+        load_t1_scale()
         load_t0(0, 0, 1)
         load_t1(0, 0, 1)
         load_w_words()
         load_t0(0, 1, 1)
-        load_bias()
         load_t1(0, 1, 3)
+        load_bias()
         load_t0(0, 2, 2)
         load_t0(1, 0, 2)
         load_t0(1, 2, 2)
@@ -344,8 +345,7 @@ def tile_bilinear_w4_kernel(tc, tensor0, tensor1_bytes, tensor1_scale, kernel_wo
         quantize("t0", 1, 0)
         for c in range(4):
             scores(0, (2 * c, 2 * c + 1), HALF, HALF)
-            multiply_q(1, c, 0)
-            multiply_q(1, c, 1)
+            both_q(1, c)
             if c + 2 < 4:
                 turn_t0(1, c + 2)
             if c == 2:
@@ -363,30 +363,33 @@ def tile_bilinear_w4_kernel(tc, tensor0, tensor1_bytes, tensor1_scale, kernel_wo
                 quantize("t1", 1, 0)
             empty_q(1, c, 0, False)
             empty_q(1, c, 1, False)
-            finish(0, 2 * c + 1, HALF, HALF, True)
+            finish(0, 2 * c + 1, HALF, HALF, c % 2 == 0)
             if c == 3:
                 quantize("q", 1, 3)
             widen_t1(1, c // 2, c % 2)
         for g in range(4):
-            scores(1, (2 * g, 2 * g + 1), 0, HALF)
-            scores(1, (2 * g, 2 * g + 1), HALF, HALF)
-            if g + 1 < 4:
+            first, second = 2 * g, 2 * g + 1
+            scores(1, (first,), 0, HALF)
+            scores(1, (first,), HALF, HALF)
+            if g < 3:
                 turn_t1(1, g + 1)
-            empty_score(1, 2 * g, 0, HALF, False)
-            empty_score(1, 2 * g + 1, 0, HALF, True)
-            empty_score(1, 2 * g, HALF, HALF, False)
-            if g == 0:
-                store(1, 0, 0, N)
-            empty_score(1, 2 * g + 1, HALF, HALF, True)
-            if g == 0:
-                store(1, 1, 0, N)
-            else:
-                store(1, 2 * g, 0, 2 * N)
-            if g + 1 < 4:
+            scores(1, (second,), 0, HALF)
+            scores(1, (second,), HALF, HALF)
+            empty_score(1, first, 0, HALF, False)
+            empty_score(1, first, HALF, HALF, True)
+            if g in (0, 3):
+                store(1, first, 0, N)
+            if g < 3:
                 empty_t1(1, g + 1, False)
-            if g + 2 < 4:
+            if g < 2:
                 widen_t1(1, g + 2, 0)
-            if g + 1 < 4:
+            if g < 3:
                 quantize("t1", 1, g + 1)
-            if g + 2 < 4:
+            empty_score(1, second, 0, HALF, False)
+            if g < 2:
                 widen_t1(1, g + 2, 1)
+            empty_score(1, second, HALF, HALF, g >= 2)
+            if g in (0, 3):
+                store(1, second, 0, N)
+            else:
+                store(1, first, 0, 2 * N)

from contextlib import ExitStack

import concourse.mybir as mybir
from concourse.masks import make_identity

F32 = mybir.dt.float32
BF16 = mybir.dt.bfloat16
I32 = mybir.dt.int32
U32 = mybir.dt.uint32
U16 = mybir.dt.uint16
U8 = mybir.dt.uint8
FP8 = mybir.dt.float8_e4m3fn
FP8X4 = mybir.dt.float8_e4m3fn_x4
FP4X4 = mybir.dt.float4_e2m1fn_x4
ALU = mybir.AluOpType
ACT = mybir.ActivationFunctionType

B, S, N, D = 2, 2, 1024, 512
P = 128
PACK = 4
ROWS = N // P
QUARTER = 256
HALF = 512
FLOPS = 2 * S * N * D * D + 2 * S * N * N * D


def tile_bilinear_w4_kernel(tc, tensor0, tensor1_bytes, tensor1_scale, kernel_words, kernel_scales, bias, out):
    nc = tc.nc
    with ExitStack() as ctx:
        keep = ctx.enter_context(tc.tile_pool(name="keep", bufs=1))
        work = ctx.enter_context(tc.tile_pool(name="work", bufs=4))
        psum = ctx.enter_context(tc.psum_pool(name="psum", bufs=8))
        ctx.enter_context(tc.manual_schedule())

        t0_rows, t1_rows = {}, {}

        def load_t0(s, first, count):
            raw = keep.tile([P, count, 2, D], BF16, name="t0_raw_%d_%d" % (s, first))
            rows = tensor0[s, first * QUARTER : (first + count) * QUARTER, :]
            nc.sync.dma_start(out=raw[:], in_=rows.rearrange("(c p r) e -> p c r e", p=P, r=2))
            for c in range(count):
                t0_rows[(s, first + c)] = raw[:, c, :, :]

        def load_t1(s, first, count):
            raw = keep.tile([P, count, 2, D], U8, name="t1_bytes_%d_%d" % (s, first))
            rows = tensor1_bytes[s].rearrange("(g p r) d -> p g r d", p=P, r=2)
            nc.sync.dma_start(out=raw[:], in_=rows[:, first : first + count, :, :])
            for g in range(count):
                t1_rows[(s, first + g)] = raw[:, g, :, :]

        w_scale_rows = keep.tile([4, 4, D // 4], I32, name="w_scale_rows")
        t1_scale = keep.tile([P, PACK], F32, name="t1_scale")
        w_words_raw = keep.tile([P, D // 2], I32, name="w_words_raw")
        bias_bf16 = keep.tile([P, 1], BF16, name="bias_bf16")
        identity = keep.tile([P, P], F32, name="identity")
        w_scale_spread = keep.tile([P, D // 4], I32, name="w_scale_spread")
        w_scales = keep.tile([P, D], U8, name="w_scales", align_bytes=64)
        w_words = keep.tile([P, D], U16, name="w_words", align_bytes=64)
        t1_scale_row = keep.tile([P, D], F32, name="t1_scale_row")

        def load_w_scales():
            nc.sync.dma_start(out=w_scale_rows[:], in_=kernel_scales[0].bitcast(I32).rearrange("(q r) n -> r q n", r=4))

        def load_t1_scale():
            nc.sync.dma_start(out=t1_scale[:], in_=tensor1_scale.rearrange("a b (p t) -> p (a b t)", t=PACK))

        def load_w_words():
            nc.sync.dma_start(out=w_words_raw[:], in_=kernel_words[0].bitcast(I32))

        def load_bias():
            nc.sync.dma_start(out=bias_bf16[:], in_=bias.partition_broadcast(P))

        def order_w_scales():
            nc.vector.memset(w_scale_spread[:], 0)
            for q in range(4):
                nc.vector.tensor_copy(out=w_scale_spread[32 * q : 32 * q + 4, :], in_=w_scale_rows[:, q, :])
            nc.vector.tensor_copy(
                out=w_scales[:].rearrange("p (t m) -> p m t", t=PACK),
                in_=w_scale_spread[:].bitcast(U8).rearrange("p (m t) -> p m t", t=PACK),
            )

        def order_w_words():
            nc.scalar.copy(
                out=w_words[:].rearrange("p (t m) -> p t m", t=PACK),
                in_=w_words_raw[:].bitcast(U16).rearrange("p (m t) -> p t m", t=PACK),
            )

        def spread_t1_scale():
            bank = psum.tile([P, HALF], F32, name="bank")
            for t in range(PACK):
                nc.tensor.transpose(bank[:, t * P : (t + 1) * P], t1_scale[:, t : t + 1].to_broadcast([P, P]), identity[:])
            nc.scalar.activation(
                out=t1_scale_row[:].rearrange("p (u n e) -> p u n e", u=2, e=2),
                in_=bank[:].rearrange("p (u e n) -> p u n e", u=2, e=2),
                func=ACT.Identity,
            )

        banks, grouped, wide = {}, {}, {}
        codes, scales = {}, {}
        for s in range(S):
            for name in ("t0", "t1", "q"):
                for h in range(2):
                    codes[(name, s, h)] = keep.tile([P, HALF], U32, name="%s_codes_%d_%d" % (name, s, h), align_bytes=64)
                    scales[(name, s, h)] = keep.tile([P, HALF], U8, name="%s_scales_%d_%d" % (name, s, h), align_bytes=64)
        result = {}
        for s in range(S):
            result[s] = keep.tile([P, ROWS * N], F32, name="result_%d" % s)

        def operand(name, s, first, count):
            h, cols = first // HALF, slice(first % HALF, first % HALF + count)
            return codes[(name, s, h)][:, cols].bitcast(FP8X4), scales[(name, s, h)][:, cols]

        def copy_out(on_vector, dst, src):
            if on_vector:
                nc.vector.tensor_copy(out=dst, in_=src)
            else:
                nc.scalar.copy(out=dst, in_=src)

        def quantize(name, s, c, first=0, count=QUARTER):
            words, exps = operand(name, s, c * QUARTER + first, count)
            nc.vector.quantize_mx(out=words, scales=exps, in_=grouped[(name, s, c)][:, first * PACK : (first + count) * PACK])

        def multiply_pair(first, count):
            bank = psum.tile([P, HALF], F32, name="bank")
            banks[("pair", first)] = bank
            q_words, q_exps = operand("q", 0, first, count)
            for r in range(2):
                t1_words, t1_exps = operand("t1", 0, r * P, P)
                nc.tensor.matmul_mx(
                    out=bank[:, r * count : (r + 1) * count],
                    lhsT=t1_words,
                    lhsT_scale=t1_exps,
                    rhs=q_words,
                    rhs_scale=q_exps,
                    start=True,
                    stop=True,
                )

        def finish_pair(first, count, on_vector):
            tile = keep.tile([P, 2 * count], F32, name="pair_result_%d" % first)
            dst = tile[:]
            src = banks[("pair", first)][:, 0 : 2 * count]
            if on_vector:
                nc.vector.tensor_scalar_add(out=dst, in0=src, scalar1=bias_bf16[:])
            else:
                nc.scalar.activation(out=dst, in_=src, func=ACT.Identity, bias=bias_bf16[:])
            rows = out[:, 0].rearrange("b (p r) j -> p r b j", r=ROWS)
            for r in range(2):
                nc.sync.dma_start(
                    out=rows[:, r, :, first : first + count],
                    in_=tile[:, r * count : (r + 1) * count].unsqueeze(1).to_broadcast([P, B, count]),
                )

        def turn_t0(s, c):
            bank = psum.tile([P, HALF], F32, name="bank")
            banks[("t0", s, c)] = bank
            words = t0_rows[(s, c)].bitcast(F32)
            for r in range(2):
                for u in range(2):
                    k = 2 * r + u
                    nc.tensor.transpose(bank[:, k * P : (k + 1) * P], words[:, r, u : D // 2 : 2], identity[:])

        def empty_t0(s, c, on_vector):
            tile = work.tile([P, QUARTER * PACK], BF16, name="t0_grouped", align_bytes=64)
            grouped[("t0", s, c)] = tile
            copy_out(
                on_vector,
                tile[:].bitcast(F32).rearrange("q (p r u) -> q p r u", r=2, u=2),
                banks[("t0", s, c)][:].rearrange("q (r u p) -> q p r u", r=2, u=2),
            )

        def widen_t1(s, g, r):
            if r == 0:
                wide[(s, g)] = work.tile([P, 2, D], BF16, name="t1_wide", align_bytes=64)
            nc.vector.tensor_tensor(
                out=wide[(s, g)][:, r, :].rearrange("p (u n e) -> p u n e", u=2, e=2),
                in0=t1_rows[(s, g)][:, r, :].bitcast(FP8).rearrange("p (n u e) -> p u n e", u=2, e=2),
                in1=t1_scale_row[:].rearrange("p (u n e) -> p u n e", u=2, e=2),
                op=ALU.mult,
            )

        def turn_t1(s, g):
            bank = psum.tile([P, HALF], F32, name="bank")
            banks[("t1", s, g)] = bank
            words = wide[(s, g)][:].bitcast(F32)
            for r in range(2):
                for u in range(2):
                    k = 2 * r + u
                    nc.tensor.transpose(bank[:, k * P : (k + 1) * P], words[:, r, u * P : (u + 1) * P], identity[:])

        def empty_t1(s, g, on_vector):
            tile = work.tile([P, QUARTER * PACK], BF16, name="t1_grouped", align_bytes=64)
            grouped[("t1", s, g)] = tile
            copy_out(
                on_vector,
                tile[:].bitcast(F32).rearrange("q (r p u) -> q r p u", r=2, u=2),
                banks[("t1", s, g)][:].rearrange("q (r u p) -> q r p u", r=2, u=2),
            )

        def multiply_q(s, c, b):
            bank = psum.tile([P, HALF], F32, name="bank")
            banks[("q", s, c, b)] = bank
            words, exps = operand("t0", s, c * QUARTER + b * P, P)
            for t in range(PACK):
                nc.tensor.matmul_mx(
                    out=bank[:, t * P : (t + 1) * P],
                    lhsT=w_words[:, t * P : (t + 1) * P].bitcast(FP4X4),
                    lhsT_scale=w_scales[:, t * P : (t + 1) * P],
                    rhs=words,
                    rhs_scale=exps,
                    start=True,
                    stop=True,
                )

        def empty_q(s, c, b, on_vector):
            if b == 0:
                grouped[("q", s, c)] = work.tile([P, QUARTER * PACK], BF16, name="q_grouped", align_bytes=64)
            copy_out(
                on_vector,
                grouped[("q", s, c)][:, b * HALF : (b + 1) * HALF].rearrange("p (j t) -> p j t", t=PACK),
                banks[("q", s, c, b)][:].rearrange("p (t j) -> p j t", t=PACK),
            )

        def multiply_score(s, r, first, count):
            bank = psum.tile([P, HALF], F32, name="bank")
            banks[("score", s, r, first)] = bank
            t1_words, t1_exps = operand("t1", s, r * P, P)
            q_words, q_exps = operand("q", s, first, count)
            nc.tensor.matmul_mx(
                out=bank[:, 0:count], lhsT=t1_words, lhsT_scale=t1_exps, rhs=q_words, rhs_scale=q_exps, start=True, stop=True
            )

        def empty_score(s, r, first, count, on_vector):
            dst = result[s][:, r * N + first : r * N + first + count]
            src = banks[("score", s, r, first)][:, 0:count]
            if on_vector:
                nc.vector.tensor_scalar_add(out=dst, in0=src, scalar1=bias_bf16[:])
            else:
                nc.scalar.activation(out=dst, in_=src, func=ACT.Identity, bias=bias_bf16[:])

        def store(s, r, first, count):
            rows = out[:, s].rearrange("b (g p r) j -> g p b (r j)", p=P, r=2)
            start = (r % 2) * N + first
            src = result[s][:, r * N + first : r * N + first + count]
            nc.sync.dma_start(out=rows[r // 2, :, :, start : start + count], in_=src.unsqueeze(1).to_broadcast([P, B, count]))


        load_w_scales()
        load_t1_scale()
        load_t0(0, 0, 1)
        load_t1(0, 0, 1)
        load_w_words()
        load_t0(0, 1, 1)
        load_t1(0, 1, 3)
        load_bias()
        load_t0(0, 2, 2)
        load_t0(1, 0, 2)
        load_t0(1, 2, 2)
        load_t1(1, 0, 4)
        make_identity(nc, identity[:])
        order_w_scales()
        spread_t1_scale()

        def scores(s, rows, first, count):
            for r in rows:
                multiply_score(s, r, first, count)

        def finish(s, r, first, count, on_vector):
            empty_score(s, r, first, count, on_vector)
            store(s, r, first, count)

        def both_q(s, c):
            multiply_q(s, c, 0)
            multiply_q(s, c, 1)

        def widen_pair(s, g):
            widen_t1(s, g, 0)
            widen_t1(s, g, 1)

        turn_t0(0, 0)
        empty_t0(0, 0, False)
        order_w_words()
        widen_pair(0, 0)
        quantize("t0", 0, 0)
        turn_t0(0, 1)
        turn_t1(0, 0)
        widen_pair(0, 1)
        empty_t0(0, 1, False)
        empty_t1(0, 0, False)
        both_q(0, 0)
        quantize("t0", 0, 1)
        quantize("t1", 0, 0)
        both_q(0, 1)
        empty_q(0, 0, 0, True)
        empty_q(0, 0, 1, False)
        quantize("q", 0, 0)
        widen_t1(0, 2, 0)
        empty_q(0, 1, 0, False)
        empty_q(0, 1, 1, True)
        scores(0, (0, 1), 0, QUARTER)
        turn_t1(0, 1)
        turn_t0(0, 2)
        finish(0, 0, 0, QUARTER, False)
        finish(0, 1, 0, QUARTER, False)
        quantize("q", 0, 1)
        empty_t1(0, 1, False)
        widen_t1(0, 2, 1)
        scores(0, (0, 1), QUARTER, QUARTER)
        turn_t1(0, 2)
        quantize("t1", 0, 1)
        empty_t0(0, 2, False)
        finish(0, 0, QUARTER, QUARTER, False)
        finish(0, 1, QUARTER, QUARTER, False)
        scores(0, (2, 3), 0, HALF)
        turn_t0(0, 3)
        widen_t1(0, 3, 0)
        quantize("t0", 0, 2)
        empty_t1(0, 2, False)
        finish(0, 2, 0, HALF, True)
        finish(0, 3, 0, HALF, False)
        quantize("t1", 0, 2)
        widen_t1(0, 3, 1)
        both_q(0, 2)
        empty_t0(0, 3, False)
        scores(0, (4, 5), 0, HALF)
        turn_t1(0, 3)
        empty_q(0, 2, 0, False)
        quantize("t0", 0, 3)
        finish(0, 4, 0, HALF, True)
        empty_t1(0, 3, False)
        finish(0, 5, 0, HALF, True)
        empty_q(0, 2, 1, False)
        quantize("t1", 0, 3)
        both_q(0, 3)
        scores(0, (6, 7), 0, HALF)
        turn_t0(1, 0)
        turn_t0(1, 1)
        quantize("q", 0, 2)
        empty_q(0, 3, 0, False)
        empty_q(0, 3, 1, True)
        finish(0, 6, 0, HALF, False)
        quantize("q", 0, 3)
        finish(0, 7, 0, HALF, False)
        empty_t0(1, 0, True)
        quantize("t0", 1, 0)
        for c in range(4):
            scores(0, (2 * c, 2 * c + 1), HALF, HALF)
            both_q(1, c)
            if c + 2 < 4:
                turn_t0(1, c + 2)
            if c == 2:
                turn_t1(1, 0)
            if c + 1 < 4:
                empty_t0(1, c + 1, False)
            if c == 3:
                empty_t1(1, 0, False)
            finish(0, 2 * c, HALF, HALF, True)
            if c > 0:
                quantize("q", 1, c - 1)
            if c + 1 < 4:
                quantize("t0", 1, c + 1)
            if c == 3:
                quantize("t1", 1, 0)
            empty_q(1, c, 0, False)
            empty_q(1, c, 1, False)
            finish(0, 2 * c + 1, HALF, HALF, c % 2 == 0)
            if c == 3:
                quantize("q", 1, 3)
            widen_t1(1, c // 2, c % 2)
        for g in range(4):
            first, second = 2 * g, 2 * g + 1
            scores(1, (first,), 0, HALF)
            scores(1, (first,), HALF, HALF)
            if g < 3:
                turn_t1(1, g + 1)
            scores(1, (second,), 0, HALF)
            scores(1, (second,), HALF, HALF)
            empty_score(1, first, 0, HALF, False)
            empty_score(1, first, HALF, HALF, True)
            if g in (0, 3):
                store(1, first, 0, N)
            if g < 3:
                empty_t1(1, g + 1, False)
            if g < 2:
                widen_t1(1, g + 2, 0)
            if g < 3:
                quantize("t1", 1, g + 1)
            empty_score(1, second, 0, HALF, False)
            if g < 2:
                widen_t1(1, g + 2, 1)
            empty_score(1, second, HALF, HALF, g >= 2)
            if g in (0, 3):
                store(1, second, 0, N)
            else:
                store(1, first, 0, 2 * N)
